import numpy as np
import ml_dtypes


def mxq(x, axis, fmt="e4m3"):
    dtype, down = {"e4m3": (ml_dtypes.float8_e4m3fn, 7), "e5m2": (ml_dtypes.float8_e5m2, 14)}[fmt]
    v = np.moveaxis(np.asarray(x, np.float32).astype(ml_dtypes.bfloat16).astype(np.float64), axis, -1)
    blocks = v.reshape(v.shape[:-1] + (-1, 32))
    amax = np.abs(blocks).max(-1, keepdims=True)
    byte = np.maximum(np.where(amax > 0, np.frexp(amax)[1] - 1 + 127, 0) - down, 1)
    scale = np.exp2(byte - 127.0)
    codes = (blocks / scale).astype(np.float32).astype(dtype).astype(np.float64)
    return np.moveaxis((codes * scale).reshape(v.shape), -1, axis)


WIDE = False


def mx_kscale(k, group=512):
    if not WIDE:
        return np.ones(k)
    levels = np.array([20, -20, 10, -10, 0])
    if group != 512:
        return np.exp2(np.random.permutation(np.resize(levels, k // group))).repeat(group)
    a = np.random.permutation(np.resize(levels, k // 512 * 4)).reshape(k // 512, 4)
    idx = np.arange(k)
    return np.exp2(a[idx // 512, idx % 128 // 32])


BF16 = ml_dtypes.bfloat16


def bf(x):
    return np.asarray(x, np.float32).astype(BF16)


def f64(x):
    return np.asarray(x).astype(np.float64)


T, B, NJ, D, E, HD, R = 128, 4, 16, 1024, 512, 128, 128
BJ = B * NJ
TOK = T * BJ
SCALING = 2.0


def setup_inputs():
    sb = mx_kscale(T * B, 512 // NJ).reshape(T, B)
    s = np.repeat(sb, NJ, axis=1)[:, :, None]
    query = np.random.standard_normal((T, BJ, D)) * s
    m = np.random.standard_normal((B, T, D)) * sb.T[:, :, None]
    w_q = np.random.standard_normal((E, D)) * 0.8 / np.sqrt(D)
    b_q = np.random.standard_normal(E) * 0.2
    A_q = np.random.standard_normal((R, D)) / np.sqrt(D)
    B_q = np.random.standard_normal((E, R)) * 0.3 / np.sqrt(R)
    g = np.random.standard_normal((T, BJ, E)) * np.exp2(np.random.randint(-12, 1, (T, BJ, 1))) * 0.25 / s
    return {"query": bf(query), "m": bf(m), "w_q": bf(w_q), "b_q": bf(b_q),
            "A_q": bf(A_q), "B_q": bf(B_q), "grad_out": bf(g)}


def reference(query, m, w_q, b_q, A_q, B_q, grad_out):
    m_exp = np.broadcast_to(f64(m).transpose(1, 0, 2)[:, :, None, :], (T, B, NJ, D)).reshape(T, BJ, D)
    q_in = (f64(query) + m_exp).reshape(TOK, D)
    g = f64(grad_out).reshape(TOK, E)
    return mxq(g, 0, "e5m2").T @ mxq(q_in, 0, "e4m3")

@@ -1,0 +1,137 @@
+import concourse.mybir as mybir
+
+FLOPS = 2 * 8192 * 512 * 1024
+BYTES = 2 * (8192 * 1024 + 512 * 1024 + 8192 * 512) + 4 * 512 * 1024
+
+BF16 = mybir.dt.bfloat16
+F32 = mybir.dt.float32
+U32 = mybir.dt.uint32
+U8 = mybir.dt.uint8
+E4M3_X4 = mybir.dt.float8_e4m3fn_x4
+E5M2_X4 = mybir.dt.float8_e5m2_x4
+
+P = 128
+PACK = 4
+K_PASS = P * PACK
+FRAMES, BATCH, JOINTS = 128, 4, 16
+D = 1024
+E = 512
+PASSES = FRAMES * BATCH * JOINTS // K_PASS
+FRAMES_PER_PASS = FRAMES // PASSES
+SHARERS = JOINTS // PACK
+E_TILE = P
+D_TILE = 512
+RUN = 4
+LOAD_AHEAD = 4
+VECTOR_COLS = 384
+
+
+def regroup(copy, grouped, rows):
+    copy(
+        out=grouped.rearrange("p (c i) j -> p c j i", i=RUN),
+        in_=rows.rearrange("p j (c i) -> p c j i", i=RUN),
+    )
+
+
+def tile_inversiontemporalmha_pa_t_kernel(tc, query, m, w_q, b_q, A_q, B_q, grad_out, out):
+    nc = tc.nc
+    q_rows = query.rearrange("t s d -> (t s) d")
+    g_rows = grad_out.rearrange("t s e -> (t s) e")
+
+    with tc.tile_pool(name="loads", bufs=LOAD_AHEAD) as loads, tc.tile_pool(
+        name="work", bufs=3
+    ) as work, tc.tile_pool(name="mx", bufs=3) as mx, tc.tile_pool(
+        name="results", bufs=4
+    ) as results, tc.psum_pool(name="sums", bufs=1) as sums:
+        acc = {}
+        for ei in range(E // E_TILE):
+            for di in range(D // D_TILE):
+                acc[(ei, di)] = sums.tile([E_TILE, D_TILE], F32, name="acc_%d_%d" % (ei, di))
+
+        def load(c):
+            tokens = slice(c * K_PASS, (c + 1) * K_PASS)
+            frames = slice(c * FRAMES_PER_PASS, (c + 1) * FRAMES_PER_PASS)
+            m_rep = loads.tile([P, D], BF16)
+            for r in range(SHARERS):
+                nc.sync.dma_start(
+                    out=m_rep[r:P:SHARERS, :], in_=m[:, frames, :].rearrange("b t d -> t b d")
+                )
+            q_raw = loads.tile([P, PACK, D], BF16)
+            nc.sync.dma_start(out=q_raw[:], in_=q_rows[tokens, :].rearrange("(p j) d -> p j d", j=PACK))
+            g_raw = loads.tile([P, PACK, E], BF16)
+            nc.sync.dma_start(out=g_raw[:], in_=g_rows[tokens, :].rearrange("(p j) e -> p j e", j=PACK))
+            return m_rep, q_raw, g_raw
+
+        def add_motion(m_rep, q_raw):
+            q_sum = work.tile([P, PACK, D], BF16)
+            nc.vector.tensor_tensor(
+                out=q_sum[:],
+                in0=q_raw[:],
+                in1=m_rep[:].unsqueeze(1).to_broadcast([P, PACK, D]),
+                op=mybir.AluOpType.add,
+            )
+            return q_sum
+
+        def regroup_g(g_raw):
+            g_grp = work.tile([P, E, PACK], BF16, align_bytes=64)
+            regroup(nc.scalar.copy, g_grp[:], g_raw[:])
+            return g_grp
+
+        def regroup_q(q_sum):
+            q_grp = work.tile([P, D, PACK], BF16, align_bytes=64)
+            regroup(nc.scalar.copy, q_grp[:, VECTOR_COLS:, :], q_sum[:, :, VECTOR_COLS:])
+            regroup(nc.vector.tensor_copy, q_grp[:, :VECTOR_COLS, :], q_sum[:, :, :VECTOR_COLS])
+            return q_grp
+
+        def quantise(grouped, width, fp8_x4, label):
+            codes = mx.tile([P, width], U32, align_bytes=64, name=label + "_codes")
+            scales = mx.tile([P, width], U8, align_bytes=64, name=label + "_scales")
+            nc.vector.quantize_mx(
+                out=codes[:].bitcast(fp8_x4),
+                scales=scales[:],
+                in_=grouped[:].rearrange("p c j -> p (c j)"),
+            )
+            return codes, scales
+
+        def multiply(c, g_codes, g_scales, q_codes, q_scales):
+            for ei in range(E // E_TILE):
+                e_cols = slice(ei * E_TILE, (ei + 1) * E_TILE)
+                for di in range(D // D_TILE):
+                    d_cols = slice(di * D_TILE, (di + 1) * D_TILE)
+                    nc.tensor.matmul_mx(
+                        out=acc[(ei, di)][:],
+                        lhsT=g_codes[:, e_cols].bitcast(E5M2_X4),
+                        lhsT_scale=g_scales[:, e_cols],
+                        rhs=q_codes[:, d_cols].bitcast(E4M3_X4),
+                        rhs_scale=q_scales[:, d_cols],
+                        start=(c == 0),
+                        stop=(c == PASSES - 1),
+                    )
+
+        raw = {}
+        for c in range(LOAD_AHEAD):
+            raw[c] = load(c)
+        g_grp = regroup_g(raw[0][2])
+        q_sum = add_motion(raw[0][0], raw[0][1])
+        for c in range(PASSES):
+            if c + LOAD_AHEAD < PASSES:
+                raw[c + LOAD_AHEAD] = load(c + LOAD_AHEAD)
+            q_grp = regroup_q(q_sum)
+            g_grp_now = g_grp
+            if c + 1 < PASSES:
+                g_grp = regroup_g(raw[c + 1][2])
+                q_sum = add_motion(raw[c + 1][0], raw[c + 1][1])
+            q_codes, q_scales = quantise(q_grp, D, E4M3_X4, "q")
+            g_codes, g_scales = quantise(g_grp_now, E, E5M2_X4, "g")
+            multiply(c, g_codes, g_scales, q_codes, q_scales)
+
+        for ei in range(E // E_TILE):
+            for di in range(D // D_TILE):
+                res = results.tile([E_TILE, D_TILE], F32)
+                if di % 2 == 0:
+                    nc.vector.tensor_copy(out=res[:], in_=acc[(ei, di)][:])
+                else:
+                    nc.scalar.copy(out=res[:], in_=acc[(ei, di)][:])
+                nc.sync.dma_start(
+                    out=out[ei * E_TILE : (ei + 1) * E_TILE, di * D_TILE : (di + 1) * D_TILE], in_=res[:]
+                )

@@ -108,30 +108,32 @@ def tile_inversiontemporalmha_pa_t_kernel(tc, query, m, w_q, b_q, A_q, B_q, grad
                         stop=(c == PASSES - 1),
                     )
 
-        raw = {}
-        for c in range(LOAD_AHEAD):
-            raw[c] = load(c)
-        g_grp = regroup_g(raw[0][2])
-        q_sum = add_motion(raw[0][0], raw[0][1])
-        for c in range(PASSES):
-            if c + LOAD_AHEAD < PASSES:
-                raw[c + LOAD_AHEAD] = load(c + LOAD_AHEAD)
-            q_grp = regroup_q(q_sum)
-            g_grp_now = g_grp
-            if c + 1 < PASSES:
-                g_grp = regroup_g(raw[c + 1][2])
-                q_sum = add_motion(raw[c + 1][0], raw[c + 1][1])
-            q_codes, q_scales = quantise(q_grp, D, E4M3_X4, "q")
-            g_codes, g_scales = quantise(g_grp_now, E, E5M2_X4, "g")
-            multiply(c, g_codes, g_scales, q_codes, q_scales)
+        with tc.manual_schedule():
+            raw = {}
+            for c in range(LOAD_AHEAD):
+                raw[c] = load(c)
+            g_grp = regroup_g(raw[0][2])
+            q_sum = add_motion(raw[0][0], raw[0][1])
+            for c in range(PASSES):
+                if c + LOAD_AHEAD < PASSES:
+                    raw[c + LOAD_AHEAD] = load(c + LOAD_AHEAD)
+                q_grp = regroup_q(q_sum)
+                g_grp_now = g_grp
+                if c + 1 < PASSES:
+                    g_grp = regroup_g(raw[c + 1][2])
+                    q_sum = add_motion(raw[c + 1][0], raw[c + 1][1])
+                q_codes, q_scales = quantise(q_grp, D, E4M3_X4, "q")
+                g_codes, g_scales = quantise(g_grp_now, E, E5M2_X4, "g")
+                multiply(c, g_codes, g_scales, q_codes, q_scales)
 
-        for ei in range(E // E_TILE):
-            for di in range(D // D_TILE):
-                res = results.tile([E_TILE, D_TILE], F32)
-                if di % 2 == 0:
-                    nc.vector.tensor_copy(out=res[:], in_=acc[(ei, di)][:])
-                else:
-                    nc.scalar.copy(out=res[:], in_=acc[(ei, di)][:])
-                nc.sync.dma_start(
-                    out=out[ei * E_TILE : (ei + 1) * E_TILE, di * D_TILE : (di + 1) * D_TILE], in_=res[:]
-                )
+            for ei in range(E // E_TILE):
+                for di in range(D // D_TILE):
+                    res = results.tile([E_TILE, D_TILE], F32)
+                    if di % 2 == 0:
+                        nc.vector.tensor_copy(out=res[:], in_=acc[(ei, di)][:])
+                    else:
+                        nc.scalar.copy(out=res[:], in_=acc[(ei, di)][:])
+                    nc.sync.dma_start(
+                        out=out[ei * E_TILE : (ei + 1) * E_TILE, di * D_TILE : (di + 1) * D_TILE],
+                        in_=res[:],
+                    )

@@ -12,13 +12,14 @@ E5M2_X4 = mybir.dt.float8_e5m2_x4
 
 P = 128
 PACK = 4
-K_PASS = P * PACK
-FRAMES, BATCH, JOINTS = 128, 4, 16
+JOINTS = 16
 D = 1024
 E = 512
-PASSES = FRAMES * BATCH * JOINTS // K_PASS
-FRAMES_PER_PASS = FRAMES // PASSES
-SHARERS = JOINTS // PACK
+PARITIES = 2
+BATCH_HALVES = 2
+FAMILIES = PARITIES * BATCH_HALVES
+PASSES_PER_FAMILY = JOINTS // PACK
+PASSES = FAMILIES * PASSES_PER_FAMILY
 E_TILE = P
 D_TILE = 512
 RUN = 4
@@ -35,39 +36,44 @@ def regroup(copy, grouped, rows):
 
 def tile_inversiontemporalmha_pa_t_kernel(tc, query, m, w_q, b_q, A_q, B_q, grad_out, out):
     nc = tc.nc
-    q_rows = query.rearrange("t s d -> (t s) d")
-    g_rows = grad_out.rearrange("t s e -> (t s) e")
+    by_family = "(y par) (h bl s j) c -> par h s y bl (j c)"
+    q_view = query.rearrange(by_family, par=PARITIES, h=BATCH_HALVES, bl=2, s=PASSES_PER_FAMILY)
+    g_view = grad_out.rearrange(by_family, par=PARITIES, h=BATCH_HALVES, bl=2, s=PASSES_PER_FAMILY)
+    m_view = m.rearrange("(h bl) (y par) c -> par h y bl c", bl=2, par=PARITIES)
 
-    with tc.tile_pool(name="loads", bufs=LOAD_AHEAD) as loads, tc.tile_pool(
-        name="work", bufs=3
-    ) as work, tc.tile_pool(name="mx", bufs=3) as mx, tc.tile_pool(
-        name="results", bufs=4
-    ) as results, tc.psum_pool(name="sums", bufs=1) as sums:
+    with tc.tile_pool(name="motion", bufs=2) as motion, tc.tile_pool(
+        name="loads", bufs=LOAD_AHEAD
+    ) as loads, tc.tile_pool(name="work", bufs=3) as work, tc.tile_pool(
+        name="mx", bufs=3
+    ) as mx, tc.tile_pool(name="results", bufs=4) as results, tc.psum_pool(
+        name="sums", bufs=1
+    ) as sums:
         acc = {}
         for ei in range(E // E_TILE):
             for di in range(D // D_TILE):
                 acc[(ei, di)] = sums.tile([E_TILE, D_TILE], F32, name="acc_%d_%d" % (ei, di))
 
-        def load(c):
-            tokens = slice(c * K_PASS, (c + 1) * K_PASS)
-            frames = slice(c * FRAMES_PER_PASS, (c + 1) * FRAMES_PER_PASS)
-            m_rep = loads.tile([P, D], BF16)
-            for r in range(SHARERS):
-                nc.sync.dma_start(
-                    out=m_rep[r:P:SHARERS, :], in_=m[:, frames, :].rearrange("b t d -> t b d")
-                )
-            q_raw = loads.tile([P, PACK, D], BF16)
-            nc.sync.dma_start(out=q_raw[:], in_=q_rows[tokens, :].rearrange("(p j) d -> p j d", j=PACK))
-            g_raw = loads.tile([P, PACK, E], BF16)
-            nc.sync.dma_start(out=g_raw[:], in_=g_rows[tokens, :].rearrange("(p j) e -> p j e", j=PACK))
-            return m_rep, q_raw, g_raw
+        m_rows = {}
 
-        def add_motion(m_rep, q_raw):
+        def load(c):
+            family, s = divmod(c, PASSES_PER_FAMILY)
+            par, h = divmod(family, BATCH_HALVES)
+            if s == 0:
+                m_row = motion.tile([P, D], BF16)
+                nc.sync.dma_start(out=m_row[:], in_=m_view[par, h])
+                m_rows[family] = m_row
+            q_raw = loads.tile([P, PACK, D], BF16)
+            nc.sync.dma_start(out=q_raw[:].rearrange("p j c -> p (j c)"), in_=q_view[par, h, s])
+            g_raw = loads.tile([P, PACK, E], BF16)
+            nc.sync.dma_start(out=g_raw[:].rearrange("p j c -> p (j c)"), in_=g_view[par, h, s])
+            return m_rows[family], q_raw, g_raw
+
+        def add_motion(m_row, q_raw):
             q_sum = work.tile([P, PACK, D], BF16)
             nc.vector.tensor_tensor(
                 out=q_sum[:],
                 in0=q_raw[:],
-                in1=m_rep[:].unsqueeze(1).to_broadcast([P, PACK, D]),
+                in1=m_row[:].unsqueeze(1).to_broadcast([P, PACK, D]),
                 op=mybir.AluOpType.add,
             )
             return q_sum

@@ -22,9 +22,10 @@ PASSES_PER_FAMILY = JOINTS // PACK
 PASSES = FAMILIES * PASSES_PER_FAMILY
 E_TILE = P
 D_TILE = 512
+BANKS = (E // E_TILE) * (D // D_TILE)
 RUN = 4
 LOAD_AHEAD = 4
-VECTOR_COLS = 384
+VECTOR_COLS = 416
 
 
 def regroup(copy, grouped, rows):
@@ -45,7 +46,7 @@ def tile_inversiontemporalmha_pa_t_kernel(tc, query, m, w_q, b_q, A_q, B_q, grad
         name="loads", bufs=LOAD_AHEAD
     ) as loads, tc.tile_pool(name="work", bufs=3) as work, tc.tile_pool(
         name="mx", bufs=3
-    ) as mx, tc.tile_pool(name="results", bufs=4) as results, tc.psum_pool(
+    ) as mx, tc.tile_pool(name="results", bufs=BANKS) as results, tc.psum_pool(
         name="sums", bufs=1
     ) as sums:
         acc = {}
@@ -92,18 +93,20 @@ def tile_inversiontemporalmha_pa_t_kernel(tc, query, m, w_q, b_q, A_q, B_q, grad
         def quantise(grouped, width, fp8_x4, label):
             codes = mx.tile([P, width], U32, align_bytes=64, name=label + "_codes")
             scales = mx.tile([P, width], U8, align_bytes=64, name=label + "_scales")
-            nc.vector.quantize_mx(
-                out=codes[:].bitcast(fp8_x4),
-                scales=scales[:],
-                in_=grouped[:].rearrange("p c j -> p (c j)"),
-            )
+            for first in range(0, width, D_TILE):
+                cols = slice(first, first + D_TILE)
+                nc.vector.quantize_mx(
+                    out=codes[:, cols].bitcast(fp8_x4),
+                    scales=scales[:, cols],
+                    in_=grouped[:, cols, :].rearrange("p c j -> p (c j)"),
+                )
             return codes, scales
 
         def multiply(c, g_codes, g_scales, q_codes, q_scales):
-            for ei in range(E // E_TILE):
-                e_cols = slice(ei * E_TILE, (ei + 1) * E_TILE)
-                for di in range(D // D_TILE):
-                    d_cols = slice(di * D_TILE, (di + 1) * D_TILE)
+            for di in range(D // D_TILE):
+                d_cols = slice(di * D_TILE, (di + 1) * D_TILE)
+                for ei in range(E // E_TILE):
+                    e_cols = slice(ei * E_TILE, (ei + 1) * E_TILE)
                     nc.tensor.matmul_mx(
                         out=acc[(ei, di)][:],
                         lhsT=g_codes[:, e_cols].bitcast(E5M2_X4),
@@ -128,14 +131,14 @@ def tile_inversiontemporalmha_pa_t_kernel(tc, query, m, w_q, b_q, A_q, B_q, grad
                 if c + 1 < PASSES:
                     g_grp = regroup_g(raw[c + 1][2])
                     q_sum = add_motion(raw[c + 1][0], raw[c + 1][1])
-                q_codes, q_scales = quantise(q_grp, D, E4M3_X4, "q")
                 g_codes, g_scales = quantise(g_grp_now, E, E5M2_X4, "g")
+                q_codes, q_scales = quantise(q_grp, D, E4M3_X4, "q")
                 multiply(c, g_codes, g_scales, q_codes, q_scales)
 
-            for ei in range(E // E_TILE):
-                for di in range(D // D_TILE):
+            for di in range(D // D_TILE):
+                for ei in range(E // E_TILE):
                     res = results.tile([E_TILE, D_TILE], F32)
-                    if di % 2 == 0:
+                    if ei % 2 == 0:
                         nc.vector.tensor_copy(out=res[:], in_=acc[(ei, di)][:])
                     else:
                         nc.scalar.copy(out=res[:], in_=acc[(ei, di)][:])

@@ -24,8 +24,9 @@ E_TILE = P
 D_TILE = 512
 BANKS = (E // E_TILE) * (D // D_TILE)
 RUN = 4
-LOAD_AHEAD = 4
-VECTOR_COLS = 416
+LOAD_AHEAD = 6
+HALF = PACK // 2
+VECTOR_COLS = 400
 
 
 def regroup(copy, grouped, rows):
@@ -37,12 +38,17 @@ def regroup(copy, grouped, rows):
 
 def tile_inversiontemporalmha_pa_t_kernel(tc, query, m, w_q, b_q, A_q, B_q, grad_out, out):
     nc = tc.nc
-    by_family = "(y par) (h bl s j) c -> par h s y bl (j c)"
-    q_view = query.rearrange(by_family, par=PARITIES, h=BATCH_HALVES, bl=2, s=PASSES_PER_FAMILY)
-    g_view = grad_out.rearrange(by_family, par=PARITIES, h=BATCH_HALVES, bl=2, s=PASSES_PER_FAMILY)
+    q_view = query.rearrange(
+        "(y par) (h bl s k j) c -> par h s k y bl (j c)",
+        par=PARITIES, h=BATCH_HALVES, bl=2, s=PASSES_PER_FAMILY, j=HALF,
+    )
+    g_view = grad_out.rearrange(
+        "(y par) (h bl s j) c -> par h s y bl (j c)",
+        par=PARITIES, h=BATCH_HALVES, bl=2, s=PASSES_PER_FAMILY,
+    )
     m_view = m.rearrange("(h bl) (y par) c -> par h y bl c", bl=2, par=PARITIES)
 
-    with tc.tile_pool(name="motion", bufs=2) as motion, tc.tile_pool(
+    with tc.tile_pool(name="motion", bufs=FAMILIES) as motion, tc.tile_pool(
         name="loads", bufs=LOAD_AHEAD
     ) as loads, tc.tile_pool(name="work", bufs=3) as work, tc.tile_pool(
         name="mx", bufs=3
@@ -64,19 +70,21 @@ def tile_inversiontemporalmha_pa_t_kernel(tc, query, m, w_q, b_q, A_q, B_q, grad
                 nc.sync.dma_start(out=m_row[:], in_=m_view[par, h])
                 m_rows[family] = m_row
             q_raw = loads.tile([P, PACK, D], BF16)
-            nc.sync.dma_start(out=q_raw[:].rearrange("p j c -> p (j c)"), in_=q_view[par, h, s])
             g_raw = loads.tile([P, PACK, E], BF16)
+            nc.sync.dma_start(out=q_raw[:, :HALF, :].rearrange("p j c -> p (j c)"), in_=q_view[par, h, s, 0])
             nc.sync.dma_start(out=g_raw[:].rearrange("p j c -> p (j c)"), in_=g_view[par, h, s])
+            nc.sync.dma_start(out=q_raw[:, HALF:, :].rearrange("p j c -> p (j c)"), in_=q_view[par, h, s, 1])
             return m_rows[family], q_raw, g_raw
 
         def add_motion(m_row, q_raw):
             q_sum = work.tile([P, PACK, D], BF16)
-            nc.vector.tensor_tensor(
-                out=q_sum[:],
-                in0=q_raw[:],
-                in1=m_row[:].unsqueeze(1).to_broadcast([P, PACK, D]),
-                op=mybir.AluOpType.add,
-            )
+            for first in range(0, PACK, HALF):
+                nc.vector.tensor_tensor(
+                    out=q_sum[:, first : first + HALF, :],
+                    in0=q_raw[:, first : first + HALF, :],
+                    in1=m_row[:].unsqueeze(1).to_broadcast([P, HALF, D]),
+                    op=mybir.AluOpType.add,
+                )
             return q_sum
 
         def regroup_g(g_raw):
@@ -139,9 +147,9 @@ def tile_inversiontemporalmha_pa_t_kernel(tc, query, m, w_q, b_q, A_q, B_q, grad
                 for ei in range(E // E_TILE):
                     res = results.tile([E_TILE, D_TILE], F32)
                     if ei % 2 == 0:
-                        nc.vector.tensor_copy(out=res[:], in_=acc[(ei, di)][:])
-                    else:
                         nc.scalar.copy(out=res[:], in_=acc[(ei, di)][:])
+                    else:
+                        nc.vector.tensor_copy(out=res[:], in_=acc[(ei, di)][:])
                     nc.sync.dma_start(
                         out=out[ei * E_TILE : (ei + 1) * E_TILE, di * D_TILE : (di + 1) * D_TILE],
                         in_=res[:],

@@ -24,9 +24,8 @@ E_TILE = P
 D_TILE = 512
 BANKS = (E // E_TILE) * (D // D_TILE)
 RUN = 4
-LOAD_AHEAD = 6
-HALF = PACK // 2
-VECTOR_COLS = 400
+LOAD_AHEAD = 4
+VECTOR_COLS = 448
 
 
 def regroup(copy, grouped, rows):
@@ -38,17 +37,12 @@ def regroup(copy, grouped, rows):
 
 def tile_inversiontemporalmha_pa_t_kernel(tc, query, m, w_q, b_q, A_q, B_q, grad_out, out):
     nc = tc.nc
-    q_view = query.rearrange(
-        "(y par) (h bl s k j) c -> par h s k y bl (j c)",
-        par=PARITIES, h=BATCH_HALVES, bl=2, s=PASSES_PER_FAMILY, j=HALF,
-    )
-    g_view = grad_out.rearrange(
-        "(y par) (h bl s j) c -> par h s y bl (j c)",
-        par=PARITIES, h=BATCH_HALVES, bl=2, s=PASSES_PER_FAMILY,
-    )
+    by_family = "(y par) (h bl s j) c -> par h s y bl (j c)"
+    q_view = query.rearrange(by_family, par=PARITIES, h=BATCH_HALVES, bl=2, s=PASSES_PER_FAMILY)
+    g_view = grad_out.rearrange(by_family, par=PARITIES, h=BATCH_HALVES, bl=2, s=PASSES_PER_FAMILY)
     m_view = m.rearrange("(h bl) (y par) c -> par h y bl c", bl=2, par=PARITIES)
 
-    with tc.tile_pool(name="motion", bufs=FAMILIES) as motion, tc.tile_pool(
+    with tc.tile_pool(name="motion", bufs=2) as motion, tc.tile_pool(
         name="loads", bufs=LOAD_AHEAD
     ) as loads, tc.tile_pool(name="work", bufs=3) as work, tc.tile_pool(
         name="mx", bufs=3
@@ -70,21 +64,19 @@ def tile_inversiontemporalmha_pa_t_kernel(tc, query, m, w_q, b_q, A_q, B_q, grad
                 nc.sync.dma_start(out=m_row[:], in_=m_view[par, h])
                 m_rows[family] = m_row
             q_raw = loads.tile([P, PACK, D], BF16)
+            nc.sync.dma_start(out=q_raw[:].rearrange("p j c -> p (j c)"), in_=q_view[par, h, s])
             g_raw = loads.tile([P, PACK, E], BF16)
-            nc.sync.dma_start(out=q_raw[:, :HALF, :].rearrange("p j c -> p (j c)"), in_=q_view[par, h, s, 0])
             nc.sync.dma_start(out=g_raw[:].rearrange("p j c -> p (j c)"), in_=g_view[par, h, s])
-            nc.sync.dma_start(out=q_raw[:, HALF:, :].rearrange("p j c -> p (j c)"), in_=q_view[par, h, s, 1])
             return m_rows[family], q_raw, g_raw
 
         def add_motion(m_row, q_raw):
             q_sum = work.tile([P, PACK, D], BF16)
-            for first in range(0, PACK, HALF):
-                nc.vector.tensor_tensor(
-                    out=q_sum[:, first : first + HALF, :],
-                    in0=q_raw[:, first : first + HALF, :],
-                    in1=m_row[:].unsqueeze(1).to_broadcast([P, HALF, D]),
-                    op=mybir.AluOpType.add,
-                )
+            nc.vector.tensor_tensor(
+                out=q_sum[:],
+                in0=q_raw[:],
+                in1=m_row[:].unsqueeze(1).to_broadcast([P, PACK, D]),
+                op=mybir.AluOpType.add,
+            )
             return q_sum
 
         def regroup_g(g_raw):
@@ -147,9 +139,9 @@ def tile_inversiontemporalmha_pa_t_kernel(tc, query, m, w_q, b_q, A_q, B_q, grad
                 for ei in range(E // E_TILE):
                     res = results.tile([E_TILE, D_TILE], F32)
                     if ei % 2 == 0:
-                        nc.scalar.copy(out=res[:], in_=acc[(ei, di)][:])
-                    else:
                         nc.vector.tensor_copy(out=res[:], in_=acc[(ei, di)][:])
+                    else:
+                        nc.scalar.copy(out=res[:], in_=acc[(ei, di)][:])
                     nc.sync.dma_start(
                         out=out[ei * E_TILE : (ei + 1) * E_TILE, di * D_TILE : (di + 1) * D_TILE],
                         in_=res[:],

@@ -1,3 +1,4 @@
+import concourse.masks as masks
 import concourse.mybir as mybir
 
 FLOPS = 2 * 8192 * 512 * 1024
@@ -22,10 +23,17 @@ PASSES_PER_FAMILY = JOINTS // PACK
 PASSES = FAMILIES * PASSES_PER_FAMILY
 E_TILE = P
 D_TILE = 512
-BANKS = (E // E_TILE) * (D // D_TILE)
+E_TILES = E // E_TILE
+D_TILES = D // D_TILE
 RUN = 4
 LOAD_AHEAD = 4
-VECTOR_COLS = 448
+STAGED_PASSES = 12
+BANK_COLS = 256
+MOVE_COLS = 128
+LATE_TILE = E_TILES - 1
+CATCH_UP = 4
+VECTOR_COLS_STAGED = 96
+VECTOR_COLS_PLAIN = 448
 
 
 def regroup(copy, grouped, rows):
@@ -42,19 +50,26 @@ def tile_inversiontemporalmha_pa_t_kernel(tc, query, m, w_q, b_q, A_q, B_q, grad
     g_view = grad_out.rearrange(by_family, par=PARITIES, h=BATCH_HALVES, bl=2, s=PASSES_PER_FAMILY)
     m_view = m.rearrange("(h bl) (y par) c -> par h y bl c", bl=2, par=PARITIES)
 
-    with tc.tile_pool(name="motion", bufs=2) as motion, tc.tile_pool(
-        name="loads", bufs=LOAD_AHEAD
-    ) as loads, tc.tile_pool(name="work", bufs=3) as work, tc.tile_pool(
-        name="mx", bufs=3
-    ) as mx, tc.tile_pool(name="results", bufs=BANKS) as results, tc.psum_pool(
+    with tc.tile_pool(name="consts", bufs=1) as consts, tc.tile_pool(
+        name="motion", bufs=2
+    ) as motion, tc.tile_pool(name="loads", bufs=LOAD_AHEAD) as loads, tc.tile_pool(
+        name="halves", bufs=4
+    ) as halves, tc.tile_pool(name="grouped", bufs=2) as grouped_pool, tc.tile_pool(
+        name="keep", bufs=1
+    ) as keep, tc.tile_pool(name="results", bufs=4) as results, tc.psum_pool(
         name="sums", bufs=1
     ) as sums:
+        ident = consts.tile([P, P], BF16)
+        masks.make_identity(nc, ident[:])
+
         acc = {}
-        for ei in range(E // E_TILE):
-            for di in range(D // D_TILE):
+        for ei in range(E_TILES - 1):
+            for di in range(D_TILES):
                 acc[(ei, di)] = sums.tile([E_TILE, D_TILE], F32, name="acc_%d_%d" % (ei, di))
 
         m_rows = {}
+        m_reps = {}
+        codes = {}
 
         def load(c):
             family, s = divmod(c, PASSES_PER_FAMILY)
@@ -67,45 +82,83 @@ def tile_inversiontemporalmha_pa_t_kernel(tc, query, m, w_q, b_q, A_q, B_q, grad
             nc.sync.dma_start(out=q_raw[:].rearrange("p j c -> p (j c)"), in_=q_view[par, h, s])
             g_raw = loads.tile([P, PACK, E], BF16)
             nc.sync.dma_start(out=g_raw[:].rearrange("p j c -> p (j c)"), in_=g_view[par, h, s])
-            return m_rows[family], q_raw, g_raw
+            return q_raw, g_raw
 
-        def add_motion(m_row, q_raw):
-            q_sum = work.tile([P, PACK, D], BF16)
+        def repeat_motion(family):
+            m_rep = motion.tile([P, D_TILE, PACK], BF16)
+            nc.vector.tensor_copy(
+                out=m_rep[:],
+                in_=m_rows[family][:, :D_TILE].unsqueeze(2).to_broadcast([P, D_TILE, PACK]),
+            )
+            m_reps[family] = m_rep
+
+        def stage(q_raw):
+            banks = []
+            for b in range(D_TILE // BANK_COLS):
+                bank = sums.tile([P, BANK_COLS, PACK], BF16, name="late_%d" % b)
+                for first in range(0, BANK_COLS, MOVE_COLS):
+                    source = b * BANK_COLS + first
+                    nc.tensor.matmul(
+                        out=bank[:, first : first + MOVE_COLS, :],
+                        lhsT=ident[:],
+                        rhs=q_raw[:, :, source : source + MOVE_COLS].rearrange("p j c -> p c j"),
+                        start=True,
+                        stop=True,
+                    )
+                banks.append(bank)
+            return banks
+
+        def add_staged(c, banks, q_grp):
+            m_rep = m_reps[c // PASSES_PER_FAMILY]
+            for b, bank in enumerate(banks):
+                cols = slice(b * BANK_COLS, (b + 1) * BANK_COLS)
+                nc.vector.tensor_tensor(
+                    out=q_grp[:, cols, :], in0=bank[:], in1=m_rep[:, cols, :], op=mybir.AluOpType.add
+                )
+
+        def add_plain(c, q_raw, half):
+            cols = slice(half * D_TILE, (half + 1) * D_TILE)
+            q_sum = halves.tile([P, PACK, D_TILE], BF16)
             nc.vector.tensor_tensor(
                 out=q_sum[:],
-                in0=q_raw[:],
-                in1=m_row[:].unsqueeze(1).to_broadcast([P, PACK, D]),
+                in0=q_raw[:, :, cols],
+                in1=m_rows[c // PASSES_PER_FAMILY][:, cols].unsqueeze(1).to_broadcast([P, PACK, D_TILE]),
                 op=mybir.AluOpType.add,
             )
             return q_sum
 
         def regroup_g(g_raw):
-            g_grp = work.tile([P, E, PACK], BF16, align_bytes=64)
+            g_grp = grouped_pool.tile([P, E, PACK], BF16, align_bytes=64)
             regroup(nc.scalar.copy, g_grp[:], g_raw[:])
             return g_grp
 
-        def regroup_q(q_sum):
-            q_grp = work.tile([P, D, PACK], BF16, align_bytes=64)
-            regroup(nc.scalar.copy, q_grp[:, VECTOR_COLS:, :], q_sum[:, :, VECTOR_COLS:])
-            regroup(nc.vector.tensor_copy, q_grp[:, :VECTOR_COLS, :], q_sum[:, :, :VECTOR_COLS])
-            return q_grp
+        def regroup_q(q_grp, q_sums, vector_cols):
+            for half, q_sum in q_sums:
+                share = max(0, min(D_TILE, vector_cols - half * D_TILE))
+                first = half * D_TILE
+                if share < D_TILE:
+                    regroup(nc.scalar.copy, q_grp[:, first + share : first + D_TILE, :], q_sum[:, :, share:])
+                if share > 0:
+                    regroup(nc.vector.tensor_copy, q_grp[:, first : first + share, :], q_sum[:, :, :share])
 
-        def quantise(grouped, width, fp8_x4, label):
-            codes = mx.tile([P, width], U32, align_bytes=64, name=label + "_codes")
-            scales = mx.tile([P, width], U8, align_bytes=64, name=label + "_scales")
+        def quantise(c, grouped, width, fp8_x4, label):
+            code = keep.tile([P, width], U32, align_bytes=64, name="%s_codes_%d" % (label, c))
+            scale = keep.tile([P, width], U8, align_bytes=64, name="%s_scales_%d" % (label, c))
             for first in range(0, width, D_TILE):
                 cols = slice(first, first + D_TILE)
                 nc.vector.quantize_mx(
-                    out=codes[:, cols].bitcast(fp8_x4),
-                    scales=scales[:, cols],
+                    out=code[:, cols].bitcast(fp8_x4),
+                    scales=scale[:, cols],
                     in_=grouped[:, cols, :].rearrange("p c j -> p (c j)"),
                 )
-            return codes, scales
+            codes[(label, c)] = (code, scale)
 
-        def multiply(c, g_codes, g_scales, q_codes, q_scales):
-            for di in range(D // D_TILE):
+        def multiply(c, e_tiles):
+            g_codes, g_scales = codes[("g", c)]
+            q_codes, q_scales = codes[("q", c)]
+            for di in range(D_TILES):
                 d_cols = slice(di * D_TILE, (di + 1) * D_TILE)
-                for ei in range(E // E_TILE):
+                for ei in e_tiles:
                     e_cols = slice(ei * E_TILE, (ei + 1) * E_TILE)
                     nc.tensor.matmul_mx(
                         out=acc[(ei, di)][:],
@@ -117,26 +170,58 @@ def tile_inversiontemporalmha_pa_t_kernel(tc, query, m, w_q, b_q, A_q, B_q, grad
                         stop=(c == PASSES - 1),
                     )
 
+        def prepare(c, banks):
+            q_grp = grouped_pool.tile([P, D, PACK], BF16, align_bytes=64)
+            if c < STAGED_PASSES:
+                add_staged(c, banks, q_grp)
+            return q_grp
+
         with tc.manual_schedule():
             raw = {}
             for c in range(LOAD_AHEAD):
                 raw[c] = load(c)
-            g_grp = regroup_g(raw[0][2])
-            q_sum = add_motion(raw[0][0], raw[0][1])
+            repeat_motion(0)
+            banks = stage(raw[0][0])
+            g_grp = regroup_g(raw[0][1])
+            q_grp = prepare(0, banks)
+            banks = stage(raw[1][0])
+            q_sums = [(1, add_plain(0, raw[0][0], 1))]
+            late_done = 0
             for c in range(PASSES):
                 if c + LOAD_AHEAD < PASSES:
                     raw[c + LOAD_AHEAD] = load(c + LOAD_AHEAD)
-                q_grp = regroup_q(q_sum)
-                g_grp_now = g_grp
+                staged = c < STAGED_PASSES
+                regroup_q(q_grp, q_sums, D_TILE + VECTOR_COLS_STAGED if staged else VECTOR_COLS_PLAIN)
+                q_grp_now, g_grp_now = q_grp, g_grp
                 if c + 1 < PASSES:
-                    g_grp = regroup_g(raw[c + 1][2])
-                    q_sum = add_motion(raw[c + 1][0], raw[c + 1][1])
-                g_codes, g_scales = quantise(g_grp_now, E, E5M2_X4, "g")
-                q_codes, q_scales = quantise(q_grp, D, E4M3_X4, "q")
-                multiply(c, g_codes, g_scales, q_codes, q_scales)
+                    g_grp = regroup_g(raw[c + 1][1])
+                    q_grp = prepare(c + 1, banks)
+                    if c + 2 < STAGED_PASSES:
+                        banks = stage(raw[c + 2][0])
+                    if c + 2 == STAGED_PASSES:
+                        for di in range(D_TILES):
+                            acc[(LATE_TILE, di)] = sums.tile([E_TILE, D_TILE], F32, name="late_%d" % di)
+                    if c + 1 < STAGED_PASSES:
+                        q_sums = [(1, add_plain(c + 1, raw[c + 1][0], 1))]
+                    else:
+                        q_sums = [(half, add_plain(c + 1, raw[c + 1][0], half)) for half in range(D_TILES)]
+                    if (c + 2) % PASSES_PER_FAMILY == 0 and c + 2 < STAGED_PASSES:
+                        repeat_motion((c + 2) // PASSES_PER_FAMILY)
+                e_tiles = list(range(E_TILES - 1))
+                if c + 2 >= STAGED_PASSES:
+                    behind = range(late_done, min(late_done + CATCH_UP, c))
+                    for past in behind:
+                        multiply(past, [LATE_TILE])
+                    late_done = max(late_done, behind.stop)
+                    if late_done == c:
+                        e_tiles.append(LATE_TILE)
+                        late_done = c + 1
+                quantise(c, g_grp_now, E, E5M2_X4, "g")
+                quantise(c, q_grp_now, D, E4M3_X4, "q")
+                multiply(c, e_tiles)
 
-            for di in range(D // D_TILE):
-                for ei in range(E // E_TILE):
+            for di in range(D_TILES):
+                for ei in range(E_TILES):
                     res = results.tile([E_TILE, D_TILE], F32)
                     if ei % 2 == 0:
                         nc.vector.tensor_copy(out=res[:], in_=acc[(ei, di)][:])

@@ -56,7 +56,7 @@ def tile_inversiontemporalmha_pa_t_kernel(tc, query, m, w_q, b_q, A_q, B_q, grad
         name="halves", bufs=4
     ) as halves, tc.tile_pool(name="grouped", bufs=2) as grouped_pool, tc.tile_pool(
         name="keep", bufs=1
-    ) as keep, tc.tile_pool(name="results", bufs=4) as results, tc.psum_pool(
+    ) as keep, tc.psum_pool(
         name="sums", bufs=1
     ) as sums:
         ident = consts.tile([P, P], BF16)
@@ -99,9 +99,9 @@ def tile_inversiontemporalmha_pa_t_kernel(tc, query, m, w_q, b_q, A_q, B_q, grad
                 for first in range(0, BANK_COLS, MOVE_COLS):
                     source = b * BANK_COLS + first
                     nc.tensor.matmul(
-                        out=bank[:, first : first + MOVE_COLS, :],
+                        out=bank[:, first : first + MOVE_COLS, :].rearrange("p c j -> p j c"),
                         lhsT=ident[:],
-                        rhs=q_raw[:, :, source : source + MOVE_COLS].rearrange("p j c -> p c j"),
+                        rhs=q_raw[:, :, source : source + MOVE_COLS],
                         start=True,
                         stop=True,
                     )
@@ -221,13 +221,13 @@ def tile_inversiontemporalmha_pa_t_kernel(tc, query, m, w_q, b_q, A_q, B_q, grad
                 multiply(c, e_tiles)
 
             for di in range(D_TILES):
+                res = loads.tile([E_TILE, E_TILES, D_TILE], F32, name="q_raw")
                 for ei in range(E_TILES):
-                    res = results.tile([E_TILE, D_TILE], F32)
                     if ei % 2 == 0:
-                        nc.vector.tensor_copy(out=res[:], in_=acc[(ei, di)][:])
+                        nc.vector.tensor_copy(out=res[:, ei, :], in_=acc[(ei, di)][:])
                     else:
-                        nc.scalar.copy(out=res[:], in_=acc[(ei, di)][:])
+                        nc.scalar.copy(out=res[:, ei, :], in_=acc[(ei, di)][:])
                     nc.sync.dma_start(
                         out=out[ei * E_TILE : (ei + 1) * E_TILE, di * D_TILE : (di + 1) * D_TILE],
-                        in_=res[:],
+                        in_=res[:, ei, :],
                     )

@@ -32,7 +32,8 @@ BANK_COLS = 256
 MOVE_COLS = 128
 LATE_TILE = E_TILES - 1
 CATCH_UP = 4
-VECTOR_COLS_STAGED = 96
+VECTOR_COLS_STAGED = 0
+GPSIMD_COLS = 160
 VECTOR_COLS_PLAIN = 448
 
 
@@ -127,9 +128,19 @@ def tile_inversiontemporalmha_pa_t_kernel(tc, query, m, w_q, b_q, A_q, B_q, grad
             )
             return q_sum
 
-        def regroup_g(g_raw):
+        def regroup_g(g_raw, gpsimd_cols):
             g_grp = grouped_pool.tile([P, E, PACK], BF16, align_bytes=64)
-            regroup(nc.scalar.copy, g_grp[:], g_raw[:])
+            rest = E - gpsimd_cols
+            regroup(nc.scalar.copy, g_grp[:, :rest, :], g_raw[:, :, :rest])
+            if gpsimd_cols > 0:
+                nc.gpsimd.tensor_scalar(
+                    out=g_grp[:, rest:, :],
+                    in0=g_raw[:, :, rest:].rearrange("p j c -> p c j"),
+                    scalar1=1.0,
+                    scalar2=0.0,
+                    op0=mybir.AluOpType.mult,
+                    op1=mybir.AluOpType.add,
+                )
             return g_grp
 
         def regroup_q(q_grp, q_sums, vector_cols):
@@ -182,7 +193,7 @@ def tile_inversiontemporalmha_pa_t_kernel(tc, query, m, w_q, b_q, A_q, B_q, grad
                 raw[c] = load(c)
             repeat_motion(0)
             banks = stage(raw[0][0])
-            g_grp = regroup_g(raw[0][1])
+            g_grp = regroup_g(raw[0][1], 0)
             q_grp = prepare(0, banks)
             banks = stage(raw[1][0])
             q_sums = [(1, add_plain(0, raw[0][0], 1))]
@@ -194,7 +205,7 @@ def tile_inversiontemporalmha_pa_t_kernel(tc, query, m, w_q, b_q, A_q, B_q, grad
                 regroup_q(q_grp, q_sums, D_TILE + VECTOR_COLS_STAGED if staged else VECTOR_COLS_PLAIN)
                 q_grp_now, g_grp_now = q_grp, g_grp
                 if c + 1 < PASSES:
-                    g_grp = regroup_g(raw[c + 1][1])
+                    g_grp = regroup_g(raw[c + 1][1], GPSIMD_COLS if c + 1 < STAGED_PASSES else 0)
                     q_grp = prepare(c + 1, banks)
                     if c + 2 < STAGED_PASSES:
                         banks = stage(raw[c + 2][0])
@@ -216,8 +227,12 @@ def tile_inversiontemporalmha_pa_t_kernel(tc, query, m, w_q, b_q, A_q, B_q, grad
                     if late_done == c:
                         e_tiles.append(LATE_TILE)
                         late_done = c + 1
-                quantise(c, g_grp_now, E, E5M2_X4, "g")
-                quantise(c, q_grp_now, D, E4M3_X4, "q")
+                if c + 2 < STAGED_PASSES:
+                    quantise(c, q_grp_now, D, E4M3_X4, "q")
+                    quantise(c, g_grp_now, E, E5M2_X4, "g")
+                else:
+                    quantise(c, g_grp_now, E, E5M2_X4, "g")
+                    quantise(c, q_grp_now, D, E4M3_X4, "q")
                 multiply(c, e_tiles)
 
             for di in range(D_TILES):

@@ -10,15 +10,15 @@ U32 = mybir.dt.uint32
 U8 = mybir.dt.uint8
 E4M3_X4 = mybir.dt.float8_e4m3fn_x4
 E5M2_X4 = mybir.dt.float8_e5m2_x4
+ADD = mybir.AluOpType.add
+MULT = mybir.AluOpType.mult
 
 P = 128
 PACK = 4
 JOINTS = 16
 D = 1024
 E = 512
-PARITIES = 2
-BATCH_HALVES = 2
-FAMILIES = PARITIES * BATCH_HALVES
+FAMILIES = 4
 PASSES_PER_FAMILY = JOINTS // PACK
 PASSES = FAMILIES * PASSES_PER_FAMILY
 E_TILE = P
@@ -28,13 +28,13 @@ D_TILES = D // D_TILE
 RUN = 4
 LOAD_AHEAD = 4
 STAGED_PASSES = 12
+STAGED_FAMILIES = STAGED_PASSES // PASSES_PER_FAMILY
 BANK_COLS = 256
 MOVE_COLS = 128
 LATE_TILE = E_TILES - 1
 CATCH_UP = 4
-VECTOR_COLS_STAGED = 0
-GPSIMD_COLS = 160
 VECTOR_COLS_PLAIN = 448
+GPSIMD_COLS = 160
 
 
 def regroup(copy, grouped, rows):
@@ -46,18 +46,16 @@ def regroup(copy, grouped, rows):
 
 def tile_inversiontemporalmha_pa_t_kernel(tc, query, m, w_q, b_q, A_q, B_q, grad_out, out):
     nc = tc.nc
-    by_family = "(y par) (h bl s j) c -> par h s y bl (j c)"
-    q_view = query.rearrange(by_family, par=PARITIES, h=BATCH_HALVES, bl=2, s=PASSES_PER_FAMILY)
-    g_view = grad_out.rearrange(by_family, par=PARITIES, h=BATCH_HALVES, bl=2, s=PASSES_PER_FAMILY)
-    m_view = m.rearrange("(h bl) (y par) c -> par h y bl c", bl=2, par=PARITIES)
+    by_family = "(f p s j) c -> f s p j c"
+    q_view = query.flatten_outer_dims().rearrange(by_family, f=FAMILIES, p=P, s=PASSES_PER_FAMILY)
+    g_view = grad_out.flatten_outer_dims().rearrange(by_family, f=FAMILIES, p=P, s=PASSES_PER_FAMILY)
+    m_view = m.rearrange("b (f tl) c -> f tl b c", f=FAMILIES)
 
     with tc.tile_pool(name="consts", bufs=1) as consts, tc.tile_pool(
-        name="motion", bufs=2
-    ) as motion, tc.tile_pool(name="loads", bufs=LOAD_AHEAD) as loads, tc.tile_pool(
-        name="halves", bufs=4
-    ) as halves, tc.tile_pool(name="grouped", bufs=2) as grouped_pool, tc.tile_pool(
-        name="keep", bufs=1
-    ) as keep, tc.psum_pool(
+        name="loads", bufs=LOAD_AHEAD
+    ) as loads, tc.tile_pool(name="halves", bufs=4) as halves, tc.tile_pool(
+        name="grouped", bufs=2
+    ) as grouped_pool, tc.tile_pool(name="keep", bufs=1) as keep, tc.psum_pool(
         name="sums", bufs=1
     ) as sums:
         ident = consts.tile([P, P], BF16)
@@ -70,39 +68,70 @@ def tile_inversiontemporalmha_pa_t_kernel(tc, query, m, w_q, b_q, A_q, B_q, grad
 
         m_rows = {}
         m_reps = {}
+        q_tiles = {}
+        g_tiles = {}
         codes = {}
+
+        def load_motion(family, half):
+            m_half = consts.tile([P, D_TILE], BF16, name="m_%d_%d" % (family, half))
+            nc.sync.dma_start(out=m_half[:], in_=m_view[family][:, :, half * D_TILE : (half + 1) * D_TILE])
+            m_rows[(family, half)] = m_half
+
+        def load_query(c, pool, pieces):
+            family, s = divmod(c, PASSES_PER_FAMILY)
+            for first, width in pieces:
+                q_raw = pool.tile([P, PACK, width], BF16, name="q_raw" if width == D else "q_%d_%d" % (c, first))
+                nc.sync.dma_start(out=q_raw[:], in_=q_view[family, s][:, :, first : first + width])
+                q_tiles.setdefault(c, []).append((first, width, q_raw))
+
+        def load_grad(c):
+            family, s = divmod(c, PASSES_PER_FAMILY)
+            g_raw = loads.tile([P, PACK, E], BF16)
+            nc.sync.dma_start(out=g_raw[:], in_=g_view[family, s])
+            g_tiles[c] = g_raw
 
         def load(c):
             family, s = divmod(c, PASSES_PER_FAMILY)
-            par, h = divmod(family, BATCH_HALVES)
-            if s == 0:
-                m_row = motion.tile([P, D], BF16)
-                nc.sync.dma_start(out=m_row[:], in_=m_view[par, h])
-                m_rows[family] = m_row
-            q_raw = loads.tile([P, PACK, D], BF16)
-            nc.sync.dma_start(out=q_raw[:].rearrange("p j c -> p (j c)"), in_=q_view[par, h, s])
-            g_raw = loads.tile([P, PACK, E], BF16)
-            nc.sync.dma_start(out=g_raw[:].rearrange("p j c -> p (j c)"), in_=g_view[par, h, s])
-            return q_raw, g_raw
+            if c < PASSES:
+                if s == 0:
+                    for half in range(D_TILES):
+                        if (family, half) not in m_rows:
+                            load_motion(family, half)
+                load_query(c, loads, [(0, D)])
+            load_grad(c - 1)
 
-        def repeat_motion(family):
-            m_rep = motion.tile([P, D_TILE, PACK], BF16)
-            nc.vector.tensor_copy(
-                out=m_rep[:],
-                in_=m_rows[family][:, :D_TILE].unsqueeze(2).to_broadcast([P, D_TILE, PACK]),
-            )
+        def q_cols(c, first, width):
+            for tile_first, tile_width, q_raw in q_tiles[c]:
+                if tile_first <= first and first + width <= tile_first + tile_width:
+                    return q_raw[:, :, first - tile_first : first - tile_first + width]
+            raise ValueError("no tile holds these columns")
+
+        def repeat_motion(family, shares):
+            m_rep = consts.tile([P, D_TILE, PACK], BF16, name="m_rep_%d" % family)
+            first = 0
+            for engine, width in shares:
+                cols = slice(first, first + width)
+                repeated = m_rows[(family, 0)][:, cols].unsqueeze(2).to_broadcast([P, width, PACK])
+                if engine == "vector":
+                    nc.vector.tensor_copy(out=m_rep[:, cols, :], in_=repeated)
+                elif engine == "gpsimd":
+                    nc.gpsimd.tensor_scalar(
+                        out=m_rep[:, cols, :], in0=repeated, scalar1=1.0, scalar2=0.0, op0=MULT, op1=ADD
+                    )
+                else:
+                    nc.scalar.copy(out=m_rep[:, cols, :], in_=repeated)
+                first += width
             m_reps[family] = m_rep
 
-        def stage(q_raw):
+        def stage(c):
             banks = []
             for b in range(D_TILE // BANK_COLS):
                 bank = sums.tile([P, BANK_COLS, PACK], BF16, name="late_%d" % b)
                 for first in range(0, BANK_COLS, MOVE_COLS):
-                    source = b * BANK_COLS + first
                     nc.tensor.matmul(
                         out=bank[:, first : first + MOVE_COLS, :].rearrange("p c j -> p j c"),
                         lhsT=ident[:],
-                        rhs=q_raw[:, :, source : source + MOVE_COLS],
+                        rhs=q_cols(c, b * BANK_COLS + first, MOVE_COLS),
                         start=True,
                         stop=True,
                     )
@@ -113,22 +142,20 @@ def tile_inversiontemporalmha_pa_t_kernel(tc, query, m, w_q, b_q, A_q, B_q, grad
             m_rep = m_reps[c // PASSES_PER_FAMILY]
             for b, bank in enumerate(banks):
                 cols = slice(b * BANK_COLS, (b + 1) * BANK_COLS)
-                nc.vector.tensor_tensor(
-                    out=q_grp[:, cols, :], in0=bank[:], in1=m_rep[:, cols, :], op=mybir.AluOpType.add
-                )
+                nc.vector.tensor_tensor(out=q_grp[:, cols, :], in0=bank[:], in1=m_rep[:, cols, :], op=ADD)
 
-        def add_plain(c, q_raw, half):
-            cols = slice(half * D_TILE, (half + 1) * D_TILE)
+        def add_plain(c, half):
             q_sum = halves.tile([P, PACK, D_TILE], BF16)
             nc.vector.tensor_tensor(
                 out=q_sum[:],
-                in0=q_raw[:, :, cols],
-                in1=m_rows[c // PASSES_PER_FAMILY][:, cols].unsqueeze(1).to_broadcast([P, PACK, D_TILE]),
-                op=mybir.AluOpType.add,
+                in0=q_cols(c, half * D_TILE, D_TILE),
+                in1=m_rows[(c // PASSES_PER_FAMILY, half)][:].unsqueeze(1).to_broadcast([P, PACK, D_TILE]),
+                op=ADD,
             )
-            return q_sum
+            return half, q_sum
 
-        def regroup_g(g_raw, gpsimd_cols):
+        def regroup_g(c, gpsimd_cols):
+            g_raw = g_tiles[c]
             g_grp = grouped_pool.tile([P, E, PACK], BF16, align_bytes=64)
             rest = E - gpsimd_cols
             regroup(nc.scalar.copy, g_grp[:, :rest, :], g_raw[:, :, :rest])
@@ -138,8 +165,8 @@ def tile_inversiontemporalmha_pa_t_kernel(tc, query, m, w_q, b_q, A_q, B_q, grad
                     in0=g_raw[:, :, rest:].rearrange("p j c -> p c j"),
                     scalar1=1.0,
                     scalar2=0.0,
-                    op0=mybir.AluOpType.mult,
-                    op1=mybir.AluOpType.add,
+                    op0=MULT,
+                    op1=ADD,
                 )
             return g_grp
 
@@ -152,17 +179,25 @@ def tile_inversiontemporalmha_pa_t_kernel(tc, query, m, w_q, b_q, A_q, B_q, grad
                 if share > 0:
                     regroup(nc.vector.tensor_copy, q_grp[:, first : first + share, :], q_sum[:, :, :share])
 
-        def quantise(c, grouped, width, fp8_x4, label):
-            code = keep.tile([P, width], U32, align_bytes=64, name="%s_codes_%d" % (label, c))
-            scale = keep.tile([P, width], U8, align_bytes=64, name="%s_scales_%d" % (label, c))
-            for first in range(0, width, D_TILE):
-                cols = slice(first, first + D_TILE)
-                nc.vector.quantize_mx(
-                    out=code[:, cols].bitcast(fp8_x4),
-                    scales=scale[:, cols],
-                    in_=grouped[:, cols, :].rearrange("p c j -> p (c j)"),
-                )
-            codes[(label, c)] = (code, scale)
+        def quantise(c, label, grouped, width, fp8_x4, first):
+            if (label, c) not in codes:
+                slot = c % STAGED_PASSES
+                code = keep.tile([P, width], U32, align_bytes=64, name="%s_codes_%d" % (label, slot))
+                scale = keep.tile([P, width], U8, align_bytes=64, name="%s_scales_%d" % (label, slot))
+                codes[(label, c)] = (code, scale)
+            code, scale = codes[(label, c)]
+            cols = slice(first, first + D_TILE)
+            nc.vector.quantize_mx(
+                out=code[:, cols].bitcast(fp8_x4),
+                scales=scale[:, cols],
+                in_=grouped[:, cols, :].rearrange("p c j -> p (c j)"),
+            )
+
+        def quantise_g(c, g_grp):
+            quantise(c, "g", g_grp, E, E5M2_X4, 0)
+
+        def quantise_q(c, q_grp, half):
+            quantise(c, "q", q_grp, D, E4M3_X4, half * D_TILE)
 
         def multiply(c, e_tiles):
             g_codes, g_scales = codes[("g", c)]
@@ -181,43 +216,48 @@ def tile_inversiontemporalmha_pa_t_kernel(tc, query, m, w_q, b_q, A_q, B_q, grad
                         stop=(c == PASSES - 1),
                     )
 
-        def prepare(c, banks):
+        def sums_of(c, banks):
             q_grp = grouped_pool.tile([P, D, PACK], BF16, align_bytes=64)
             if c < STAGED_PASSES:
                 add_staged(c, banks, q_grp)
-            return q_grp
+                if c + 1 < STAGED_PASSES:
+                    banks = stage(c + 1)
+                if c + 1 == STAGED_PASSES:
+                    for di in range(D_TILES):
+                        acc[(LATE_TILE, di)] = sums.tile([E_TILE, D_TILE], F32, name="late_%d" % di)
+                q_sums = [add_plain(c, 1)]
+                quantise_q(c, q_grp, 0)
+            else:
+                q_sums = [add_plain(c, half) for half in range(D_TILES)]
+            return q_grp, q_sums, banks
 
         with tc.manual_schedule():
-            raw = {}
-            for c in range(LOAD_AHEAD):
-                raw[c] = load(c)
-            repeat_motion(0)
-            banks = stage(raw[0][0])
-            g_grp = regroup_g(raw[0][1], 0)
-            q_grp = prepare(0, banks)
-            banks = stage(raw[1][0])
-            q_sums = [(1, add_plain(0, raw[0][0], 1))]
+            for family in range(STAGED_FAMILIES):
+                load_motion(family, 0)
+            load_query(0, consts, [(0, BANK_COLS), (BANK_COLS, BANK_COLS)])
+            load_motion(0, 1)
+            load_query(0, consts, [(D_TILE, D_TILE)])
+            load_query(1, consts, [(0, D_TILE)])
+            load_grad(0)
+            load_query(1, consts, [(D_TILE, D_TILE)])
+            for c in range(2, LOAD_AHEAD):
+                load(c)
+            repeat_motion(0, [("vector", D_TILE)])
+            repeat_motion(2, [("scalar", D_TILE)])
+            repeat_motion(1, [("gpsimd", D_TILE // 2), ("scalar", D_TILE // 2)])
+            banks = stage(0)
+            q_grp, q_sums, banks = sums_of(0, banks)
+            g_grp = regroup_g(0, 0)
             late_done = 0
             for c in range(PASSES):
-                if c + LOAD_AHEAD < PASSES:
-                    raw[c + LOAD_AHEAD] = load(c + LOAD_AHEAD)
+                if c + LOAD_AHEAD <= PASSES:
+                    load(c + LOAD_AHEAD)
                 staged = c < STAGED_PASSES
-                regroup_q(q_grp, q_sums, D_TILE + VECTOR_COLS_STAGED if staged else VECTOR_COLS_PLAIN)
+                regroup_q(q_grp, q_sums, 0 if staged else VECTOR_COLS_PLAIN)
                 q_grp_now, g_grp_now = q_grp, g_grp
                 if c + 1 < PASSES:
-                    g_grp = regroup_g(raw[c + 1][1], GPSIMD_COLS if c + 1 < STAGED_PASSES else 0)
-                    q_grp = prepare(c + 1, banks)
-                    if c + 2 < STAGED_PASSES:
-                        banks = stage(raw[c + 2][0])
-                    if c + 2 == STAGED_PASSES:
-                        for di in range(D_TILES):
-                            acc[(LATE_TILE, di)] = sums.tile([E_TILE, D_TILE], F32, name="late_%d" % di)
-                    if c + 1 < STAGED_PASSES:
-                        q_sums = [(1, add_plain(c + 1, raw[c + 1][0], 1))]
-                    else:
-                        q_sums = [(half, add_plain(c + 1, raw[c + 1][0], half)) for half in range(D_TILES)]
-                    if (c + 2) % PASSES_PER_FAMILY == 0 and c + 2 < STAGED_PASSES:
-                        repeat_motion((c + 2) // PASSES_PER_FAMILY)
+                    g_grp = regroup_g(c + 1, GPSIMD_COLS if c + 1 < STAGED_PASSES else 0)
+                    q_grp, q_sums, banks = sums_of(c + 1, banks)
                 e_tiles = list(range(E_TILES - 1))
                 if c + 2 >= STAGED_PASSES:
                     behind = range(late_done, min(late_done + CATCH_UP, c))
@@ -228,11 +268,13 @@ def tile_inversiontemporalmha_pa_t_kernel(tc, query, m, w_q, b_q, A_q, B_q, grad
                         e_tiles.append(LATE_TILE)
                         late_done = c + 1
                 if c + 2 < STAGED_PASSES:
-                    quantise(c, q_grp_now, D, E4M3_X4, "q")
-                    quantise(c, g_grp_now, E, E5M2_X4, "g")
+                    quantise_q(c, q_grp_now, 1)
+                    quantise_g(c, g_grp_now)
                 else:
-                    quantise(c, g_grp_now, E, E5M2_X4, "g")
-                    quantise(c, q_grp_now, D, E4M3_X4, "q")
+                    quantise_g(c, g_grp_now)
+                    if not staged:
+                        quantise_q(c, q_grp_now, 0)
+                    quantise_q(c, q_grp_now, 1)
                 multiply(c, e_tiles)
 
             for di in range(D_TILES):

@@ -31,10 +31,10 @@ STAGED_PASSES = 12
 STAGED_FAMILIES = STAGED_PASSES // PASSES_PER_FAMILY
 BANK_COLS = 256
 MOVE_COLS = 128
-LATE_TILE = E_TILES - 1
-CATCH_UP = 4
+DEFERRED = [(3, 0), (3, 1), (2, 1)]
+CATCH_UP = 3
 VECTOR_COLS_PLAIN = 448
-GPSIMD_COLS = 160
+GPSIMD_COLS = 352
 
 
 def regroup(copy, grouped, rows):
@@ -61,13 +61,15 @@ def tile_inversiontemporalmha_pa_t_kernel(tc, query, m, w_q, b_q, A_q, B_q, grad
         ident = consts.tile([P, P], BF16)
         masks.make_identity(nc, ident[:])
 
+        out_tiles = [(ei, di) for di in range(D_TILES) for ei in range(E_TILES)]
+        early_tiles = [tile for tile in out_tiles if tile not in DEFERRED]
         acc = {}
-        for ei in range(E_TILES - 1):
-            for di in range(D_TILES):
-                acc[(ei, di)] = sums.tile([E_TILE, D_TILE], F32, name="acc_%d_%d" % (ei, di))
+        for ei, di in early_tiles:
+            acc[(ei, di)] = sums.tile([E_TILE, D_TILE], F32, name="acc_%d_%d" % (ei, di))
 
         m_rows = {}
         m_reps = {}
+        m_banks = {}
         q_tiles = {}
         g_tiles = {}
         codes = {}
@@ -123,6 +125,11 @@ def tile_inversiontemporalmha_pa_t_kernel(tc, query, m, w_q, b_q, A_q, B_q, grad
                 first += width
             m_reps[family] = m_rep
 
+        def stage_motion(family):
+            m_bank = sums.tile([P, D_TILE], BF16, name="late_2")
+            nc.tensor.matmul(out=m_bank[:], lhsT=ident[:], rhs=m_rows[(family, 1)][:], start=True, stop=True)
+            m_banks[family] = m_bank
+
         def stage(c):
             banks = []
             for b in range(D_TILE // BANK_COLS):
@@ -145,11 +152,13 @@ def tile_inversiontemporalmha_pa_t_kernel(tc, query, m, w_q, b_q, A_q, B_q, grad
                 nc.vector.tensor_tensor(out=q_grp[:, cols, :], in0=bank[:], in1=m_rep[:, cols, :], op=ADD)
 
         def add_plain(c, half):
+            family = c // PASSES_PER_FAMILY
+            m_half = m_banks[family] if c < STAGED_PASSES else m_rows[(family, half)]
             q_sum = halves.tile([P, PACK, D_TILE], BF16)
             nc.vector.tensor_tensor(
                 out=q_sum[:],
                 in0=q_cols(c, half * D_TILE, D_TILE),
-                in1=m_rows[(c // PASSES_PER_FAMILY, half)][:].unsqueeze(1).to_broadcast([P, PACK, D_TILE]),
+                in1=m_half[:].unsqueeze(1).to_broadcast([P, PACK, D_TILE]),
                 op=ADD,
             )
             return half, q_sum
@@ -199,22 +208,21 @@ def tile_inversiontemporalmha_pa_t_kernel(tc, query, m, w_q, b_q, A_q, B_q, grad
         def quantise_q(c, q_grp, half):
             quantise(c, "q", q_grp, D, E4M3_X4, half * D_TILE)
 
-        def multiply(c, e_tiles):
+        def multiply(c, tiles):
             g_codes, g_scales = codes[("g", c)]
             q_codes, q_scales = codes[("q", c)]
-            for di in range(D_TILES):
+            for ei, di in tiles:
                 d_cols = slice(di * D_TILE, (di + 1) * D_TILE)
-                for ei in e_tiles:
-                    e_cols = slice(ei * E_TILE, (ei + 1) * E_TILE)
-                    nc.tensor.matmul_mx(
-                        out=acc[(ei, di)][:],
-                        lhsT=g_codes[:, e_cols].bitcast(E5M2_X4),
-                        lhsT_scale=g_scales[:, e_cols],
-                        rhs=q_codes[:, d_cols].bitcast(E4M3_X4),
-                        rhs_scale=q_scales[:, d_cols],
-                        start=(c == 0),
-                        stop=(c == PASSES - 1),
-                    )
+                e_cols = slice(ei * E_TILE, (ei + 1) * E_TILE)
+                nc.tensor.matmul_mx(
+                    out=acc[(ei, di)][:],
+                    lhsT=g_codes[:, e_cols].bitcast(E5M2_X4),
+                    lhsT_scale=g_scales[:, e_cols],
+                    rhs=q_codes[:, d_cols].bitcast(E4M3_X4),
+                    rhs_scale=q_scales[:, d_cols],
+                    start=(c == 0),
+                    stop=(c == PASSES - 1),
+                )
 
         def sums_of(c, banks):
             q_grp = grouped_pool.tile([P, D, PACK], BF16, align_bytes=64)
@@ -222,10 +230,12 @@ def tile_inversiontemporalmha_pa_t_kernel(tc, query, m, w_q, b_q, A_q, B_q, grad
                 add_staged(c, banks, q_grp)
                 if c + 1 < STAGED_PASSES:
                     banks = stage(c + 1)
-                if c + 1 == STAGED_PASSES:
-                    for di in range(D_TILES):
-                        acc[(LATE_TILE, di)] = sums.tile([E_TILE, D_TILE], F32, name="late_%d" % di)
                 q_sums = [add_plain(c, 1)]
+                if c + 1 < STAGED_PASSES and (c + 1) % PASSES_PER_FAMILY == 0:
+                    stage_motion((c + 1) // PASSES_PER_FAMILY)
+                if c + 1 == STAGED_PASSES:
+                    for bank, tile in enumerate(DEFERRED):
+                        acc[tile] = sums.tile([E_TILE, D_TILE], F32, name="late_%d" % bank)
                 quantise_q(c, q_grp, 0)
             else:
                 q_sums = [add_plain(c, half) for half in range(D_TILES)]
@@ -246,6 +256,7 @@ def tile_inversiontemporalmha_pa_t_kernel(tc, query, m, w_q, b_q, A_q, B_q, grad
             repeat_motion(2, [("scalar", D_TILE)])
             repeat_motion(1, [("gpsimd", D_TILE // 2), ("scalar", D_TILE // 2)])
             banks = stage(0)
+            stage_motion(0)
             q_grp, q_sums, banks = sums_of(0, banks)
             g_grp = regroup_g(0, 0)
             late_done = 0
@@ -258,14 +269,14 @@ def tile_inversiontemporalmha_pa_t_kernel(tc, query, m, w_q, b_q, A_q, B_q, grad
                 if c + 1 < PASSES:
                     g_grp = regroup_g(c + 1, GPSIMD_COLS if c + 1 < STAGED_PASSES else 0)
                     q_grp, q_sums, banks = sums_of(c + 1, banks)
-                e_tiles = list(range(E_TILES - 1))
+                tiles = early_tiles
                 if c + 2 >= STAGED_PASSES:
                     behind = range(late_done, min(late_done + CATCH_UP, c))
                     for past in behind:
-                        multiply(past, [LATE_TILE])
+                        multiply(past, DEFERRED)
                     late_done = max(late_done, behind.stop)
                     if late_done == c:
-                        e_tiles.append(LATE_TILE)
+                        tiles = out_tiles
                         late_done = c + 1
                 if c + 2 < STAGED_PASSES:
                     quantise_q(c, q_grp_now, 1)
@@ -275,7 +286,7 @@ def tile_inversiontemporalmha_pa_t_kernel(tc, query, m, w_q, b_q, A_q, B_q, grad
                     if not staged:
                         quantise_q(c, q_grp_now, 0)
                     quantise_q(c, q_grp_now, 1)
-                multiply(c, e_tiles)
+                multiply(c, tiles)
 
             for di in range(D_TILES):
                 res = loads.tile([E_TILE, E_TILES, D_TILE], F32, name="q_raw")

@@ -33,7 +33,9 @@ BANK_COLS = 256
 MOVE_COLS = 128
 DEFERRED = [(3, 0), (3, 1), (2, 1)]
 CATCH_UP = 3
-VECTOR_COLS_PLAIN = 448
+VECTOR_COLS_PLAIN = 96
+AHEAD_FIRST = 4
+AHEAD_COLS = 256
 GPSIMD_COLS = 352
 
 
@@ -55,7 +57,9 @@ def tile_inversiontemporalmha_pa_t_kernel(tc, query, m, w_q, b_q, A_q, B_q, grad
         name="loads", bufs=LOAD_AHEAD
     ) as loads, tc.tile_pool(name="halves", bufs=4) as halves, tc.tile_pool(
         name="grouped", bufs=2
-    ) as grouped_pool, tc.tile_pool(name="keep", bufs=1) as keep, tc.psum_pool(
+    ) as grouped_pool, tc.tile_pool(name="ahead", bufs=2) as ahead, tc.tile_pool(
+        name="keep", bufs=1
+    ) as keep, tc.psum_pool(
         name="sums", bufs=1
     ) as sums:
         ident = consts.tile([P, P], BF16)
@@ -70,6 +74,7 @@ def tile_inversiontemporalmha_pa_t_kernel(tc, query, m, w_q, b_q, A_q, B_q, grad
         m_rows = {}
         m_reps = {}
         m_banks = {}
+        g_late = {}
         q_tiles = {}
         g_tiles = {}
         codes = {}
@@ -79,16 +84,26 @@ def tile_inversiontemporalmha_pa_t_kernel(tc, query, m, w_q, b_q, A_q, B_q, grad
             nc.sync.dma_start(out=m_half[:], in_=m_view[family][:, :, half * D_TILE : (half + 1) * D_TILE])
             m_rows[(family, half)] = m_half
 
+        def q_name(c, first, width):
+            if width == D:
+                return "q_raw"
+            if width == BANK_COLS:
+                return "q_bank_%d" % (first // BANK_COLS)
+            return "spare_%d" % (D_TILES * c + first // D_TILE - 1)
+
         def load_query(c, pool, pieces):
             family, s = divmod(c, PASSES_PER_FAMILY)
             for first, width in pieces:
-                q_raw = pool.tile([P, PACK, width], BF16, name="q_raw" if width == D else "q_%d_%d" % (c, first))
+                q_raw = pool.tile([P, PACK, width], BF16, align_bytes=64, name=q_name(c, first, width))
                 nc.sync.dma_start(out=q_raw[:], in_=q_view[family, s][:, :, first : first + width])
                 q_tiles.setdefault(c, []).append((first, width, q_raw))
 
         def load_grad(c):
             family, s = divmod(c, PASSES_PER_FAMILY)
-            g_raw = loads.tile([P, PACK, E], BF16)
+            if c < STAGED_PASSES:
+                g_raw = loads.tile([P, PACK, E], BF16)
+            else:
+                g_raw = ahead.tile([P, PACK, E], BF16, name="g_ahead")
             nc.sync.dma_start(out=g_raw[:], in_=g_view[family, s])
             g_tiles[c] = g_raw
 
@@ -100,7 +115,8 @@ def tile_inversiontemporalmha_pa_t_kernel(tc, query, m, w_q, b_q, A_q, B_q, grad
                         if (family, half) not in m_rows:
                             load_motion(family, half)
                 load_query(c, loads, [(0, D)])
-            load_grad(c - 1)
+            if c - 1 < STAGED_PASSES:
+                load_grad(c - 1)
 
         def q_cols(c, first, width):
             for tile_first, tile_width, q_raw in q_tiles[c]:
@@ -178,6 +194,14 @@ def tile_inversiontemporalmha_pa_t_kernel(tc, query, m, w_q, b_q, A_q, B_q, grad
                     op1=ADD,
                 )
             return g_grp
+
+        def regroup_ahead(step):
+            c, first = divmod(step * AHEAD_COLS, E)
+            c += STAGED_PASSES
+            if first == 0:
+                g_late[c] = consts.tile([P, E, PACK], BF16, align_bytes=64, name="spare_%d" % (c - STAGED_PASSES))
+            cols = slice(first, first + AHEAD_COLS)
+            regroup(nc.scalar.copy, g_late[c][:, cols, :], g_tiles[c][:, :, cols])
 
         def regroup_q(q_grp, q_sums, vector_cols):
             for half, q_sum in q_sums:
@@ -263,11 +287,26 @@ def tile_inversiontemporalmha_pa_t_kernel(tc, query, m, w_q, b_q, A_q, B_q, grad
             for c in range(PASSES):
                 if c + LOAD_AHEAD <= PASSES:
                     load(c + LOAD_AHEAD)
+                steps_a_pass = E // AHEAD_COLS
+                ahead_step = c - AHEAD_FIRST
+                if 0 <= ahead_step + 2 < (PASSES - STAGED_PASSES) * steps_a_pass and (ahead_step + 2) % steps_a_pass == 0:
+                    load_grad(STAGED_PASSES + (ahead_step + 2) // steps_a_pass)
                 staged = c < STAGED_PASSES
-                regroup_q(q_grp, q_sums, 0 if staged else VECTOR_COLS_PLAIN)
+                if staged:
+                    vector_cols = 0
+                elif c + 1 < PASSES:
+                    vector_cols = VECTOR_COLS_PLAIN
+                else:
+                    vector_cols = D_TILE
+                regroup_q(q_grp, q_sums, vector_cols)
                 q_grp_now, g_grp_now = q_grp, g_grp
                 if c + 1 < PASSES:
-                    g_grp = regroup_g(c + 1, GPSIMD_COLS if c + 1 < STAGED_PASSES else 0)
+                    if c + 1 < STAGED_PASSES:
+                        g_grp = regroup_g(c + 1, GPSIMD_COLS)
+                    else:
+                        g_grp = g_late[c + 1]
+                    if 0 <= ahead_step < (PASSES - STAGED_PASSES) * steps_a_pass:
+                        regroup_ahead(ahead_step)
                     q_grp, q_sums, banks = sums_of(c + 1, banks)
                 tiles = early_tiles
                 if c + 2 >= STAGED_PASSES:
@@ -289,7 +328,7 @@ def tile_inversiontemporalmha_pa_t_kernel(tc, query, m, w_q, b_q, A_q, B_q, grad
                 multiply(c, tiles)
 
             for di in range(D_TILES):
-                res = loads.tile([E_TILE, E_TILES, D_TILE], F32, name="q_raw")
+                res = loads.tile([E_TILE, E_TILES, D_TILE], F32, align_bytes=64, name="q_raw")
                 for ei in range(E_TILES):
                     if ei % 2 == 0:
                         nc.vector.tensor_copy(out=res[:, ei, :], in_=acc[(ei, di)][:])

@@ -26,6 +26,7 @@ D_TILE = 512
 E_TILES = E // E_TILE
 D_TILES = D // D_TILE
 RUN = 4
+SCALAR_RUN = 8
 LOAD_AHEAD = 4
 STAGED_PASSES = 12
 STAGED_FAMILIES = STAGED_PASSES // PASSES_PER_FAMILY
@@ -39,10 +40,10 @@ AHEAD_COLS = 256
 GPSIMD_COLS = 352
 
 
-def regroup(copy, grouped, rows):
+def regroup(copy, grouped, rows, run):
     copy(
-        out=grouped.rearrange("p (c i) j -> p c j i", i=RUN),
-        in_=rows.rearrange("p j (c i) -> p c j i", i=RUN),
+        out=grouped.rearrange("p (c i) j -> p c j i", i=run),
+        in_=rows.rearrange("p j (c i) -> p c j i", i=run),
     )
 
 
@@ -183,7 +184,7 @@ def tile_inversiontemporalmha_pa_t_kernel(tc, query, m, w_q, b_q, A_q, B_q, grad
             g_raw = g_tiles[c]
             g_grp = grouped_pool.tile([P, E, PACK], BF16, align_bytes=64)
             rest = E - gpsimd_cols
-            regroup(nc.scalar.copy, g_grp[:, :rest, :], g_raw[:, :, :rest])
+            regroup(nc.scalar.copy, g_grp[:, :rest, :], g_raw[:, :, :rest], SCALAR_RUN)
             if gpsimd_cols > 0:
                 nc.gpsimd.tensor_scalar(
                     out=g_grp[:, rest:, :],
@@ -201,16 +202,16 @@ def tile_inversiontemporalmha_pa_t_kernel(tc, query, m, w_q, b_q, A_q, B_q, grad
             if first == 0:
                 g_late[c] = consts.tile([P, E, PACK], BF16, align_bytes=64, name="spare_%d" % (c - STAGED_PASSES))
             cols = slice(first, first + AHEAD_COLS)
-            regroup(nc.scalar.copy, g_late[c][:, cols, :], g_tiles[c][:, :, cols])
+            regroup(nc.scalar.copy, g_late[c][:, cols, :], g_tiles[c][:, :, cols], SCALAR_RUN)
 
         def regroup_q(q_grp, q_sums, vector_cols):
             for half, q_sum in q_sums:
                 share = max(0, min(D_TILE, vector_cols - half * D_TILE))
                 first = half * D_TILE
                 if share < D_TILE:
-                    regroup(nc.scalar.copy, q_grp[:, first + share : first + D_TILE, :], q_sum[:, :, share:])
+                    regroup(nc.scalar.copy, q_grp[:, first + share : first + D_TILE, :], q_sum[:, :, share:], SCALAR_RUN)
                 if share > 0:
-                    regroup(nc.vector.tensor_copy, q_grp[:, first : first + share, :], q_sum[:, :, :share])
+                    regroup(nc.vector.tensor_copy, q_grp[:, first : first + share, :], q_sum[:, :, :share], RUN)
 
         def quantise(c, label, grouped, width, fp8_x4, first):
             if (label, c) not in codes:

import concourse.masks as masks
import concourse.mybir as mybir

FLOPS = 2 * 8192 * 512 * 1024
BYTES = 2 * (8192 * 1024 + 512 * 1024 + 8192 * 512) + 4 * 512 * 1024

BF16 = mybir.dt.bfloat16
F32 = mybir.dt.float32
U32 = mybir.dt.uint32
U8 = mybir.dt.uint8
E4M3_X4 = mybir.dt.float8_e4m3fn_x4
E5M2_X4 = mybir.dt.float8_e5m2_x4
ADD = mybir.AluOpType.add
MULT = mybir.AluOpType.mult

P = 128
PACK = 4
JOINTS = 16
D = 1024
E = 512
FAMILIES = 4
PASSES_PER_FAMILY = JOINTS // PACK
PASSES = FAMILIES * PASSES_PER_FAMILY
E_TILE = P
D_TILE = 512
E_TILES = E // E_TILE
D_TILES = D // D_TILE
RUN = 4
SCALAR_RUN = 8
LOAD_AHEAD = 4
STAGED_PASSES = 12
STAGED_FAMILIES = STAGED_PASSES // PASSES_PER_FAMILY
BANK_COLS = 256
MOVE_COLS = 128
DEFERRED = [(3, 0), (3, 1), (2, 1)]
CATCH_UP = 3
VECTOR_COLS_PLAIN = 96
AHEAD_FIRST = 4
AHEAD_COLS = 256
GPSIMD_COLS = 352


def regroup(copy, grouped, rows, run):
    copy(
        out=grouped.rearrange("p (c i) j -> p c j i", i=run),
        in_=rows.rearrange("p j (c i) -> p c j i", i=run),
    )


def tile_inversiontemporalmha_pa_t_kernel(tc, query, m, w_q, b_q, A_q, B_q, grad_out, out):
    nc = tc.nc
    by_family = "(f p s j) c -> f s p j c"
    q_view = query.flatten_outer_dims().rearrange(by_family, f=FAMILIES, p=P, s=PASSES_PER_FAMILY)
    g_view = grad_out.flatten_outer_dims().rearrange(by_family, f=FAMILIES, p=P, s=PASSES_PER_FAMILY)
    m_view = m.rearrange("b (f tl) c -> f tl b c", f=FAMILIES)

    with tc.tile_pool(name="consts", bufs=1) as consts, tc.tile_pool(
        name="loads", bufs=LOAD_AHEAD
    ) as loads, tc.tile_pool(name="halves", bufs=4) as halves, tc.tile_pool(
        name="grouped", bufs=2
    ) as grouped_pool, tc.tile_pool(name="ahead", bufs=2) as ahead, tc.tile_pool(
        name="keep", bufs=1
    ) as keep, tc.psum_pool(
        name="sums", bufs=1
    ) as sums:
        ident = consts.tile([P, P], BF16)
        masks.make_identity(nc, ident[:])

        out_tiles = [(ei, di) for di in range(D_TILES) for ei in range(E_TILES)]
        early_tiles = [tile for tile in out_tiles if tile not in DEFERRED]
        acc = {}
        for ei, di in early_tiles:
            acc[(ei, di)] = sums.tile([E_TILE, D_TILE], F32, name="acc_%d_%d" % (ei, di))

        m_rows = {}
        m_reps = {}
        m_banks = {}
        g_late = {}
        q_tiles = {}
        g_tiles = {}
        codes = {}

        def load_motion(family, half):
            m_half = consts.tile([P, D_TILE], BF16, name="m_%d_%d" % (family, half))
            nc.sync.dma_start(out=m_half[:], in_=m_view[family][:, :, half * D_TILE : (half + 1) * D_TILE])
            m_rows[(family, half)] = m_half

        def q_name(c, first, width):
            if width == D:
                return "q_raw"
            if width == BANK_COLS:
                return "q_bank_%d" % (first // BANK_COLS)
            return "spare_%d" % (D_TILES * c + first // D_TILE - 1)

        def load_query(c, pool, pieces):
            family, s = divmod(c, PASSES_PER_FAMILY)
            for first, width in pieces:
                q_raw = pool.tile([P, PACK, width], BF16, align_bytes=64, name=q_name(c, first, width))
                nc.sync.dma_start(out=q_raw[:], in_=q_view[family, s][:, :, first : first + width])
                q_tiles.setdefault(c, []).append((first, width, q_raw))

        def load_grad(c):
            family, s = divmod(c, PASSES_PER_FAMILY)
            if c < STAGED_PASSES:
                g_raw = loads.tile([P, PACK, E], BF16)
            else:
                g_raw = ahead.tile([P, PACK, E], BF16, name="g_ahead")
            nc.sync.dma_start(out=g_raw[:], in_=g_view[family, s])
            g_tiles[c] = g_raw

        def load(c):
            family, s = divmod(c, PASSES_PER_FAMILY)
            if c < PASSES:
                if s == 0:
                    for half in range(D_TILES):
                        if (family, half) not in m_rows:
                            load_motion(family, half)
                load_query(c, loads, [(0, D)])
            if c - 1 < STAGED_PASSES:
                load_grad(c - 1)

        def q_cols(c, first, width):
            for tile_first, tile_width, q_raw in q_tiles[c]:
                if tile_first <= first and first + width <= tile_first + tile_width:
                    return q_raw[:, :, first - tile_first : first - tile_first + width]
            raise ValueError("no tile holds these columns")

        def repeat_motion(family, shares):
            m_rep = consts.tile([P, D_TILE, PACK], BF16, name="m_rep_%d" % family)
            first = 0
            for engine, width in shares:
                cols = slice(first, first + width)
                repeated = m_rows[(family, 0)][:, cols].unsqueeze(2).to_broadcast([P, width, PACK])
                if engine == "vector":
                    nc.vector.tensor_copy(out=m_rep[:, cols, :], in_=repeated)
                elif engine == "gpsimd":
                    nc.gpsimd.tensor_scalar(
                        out=m_rep[:, cols, :], in0=repeated, scalar1=1.0, scalar2=0.0, op0=MULT, op1=ADD
                    )
                else:
                    nc.scalar.copy(out=m_rep[:, cols, :], in_=repeated)
                first += width
            m_reps[family] = m_rep

        def stage_motion(family):
            m_bank = sums.tile([P, D_TILE], BF16, name="late_2")
            nc.tensor.matmul(out=m_bank[:], lhsT=ident[:], rhs=m_rows[(family, 1)][:], start=True, stop=True)
            m_banks[family] = m_bank

        def stage(c):
            banks = []
            for b in range(D_TILE // BANK_COLS):
                bank = sums.tile([P, BANK_COLS, PACK], BF16, name="late_%d" % b)
                for first in range(0, BANK_COLS, MOVE_COLS):
                    nc.tensor.matmul(
                        out=bank[:, first : first + MOVE_COLS, :].rearrange("p c j -> p j c"),
                        lhsT=ident[:],
                        rhs=q_cols(c, b * BANK_COLS + first, MOVE_COLS),
                        start=True,
                        stop=True,
                    )
                banks.append(bank)
            return banks

        def add_staged(c, banks, q_grp):
            m_rep = m_reps[c // PASSES_PER_FAMILY]
            for b, bank in enumerate(banks):
                cols = slice(b * BANK_COLS, (b + 1) * BANK_COLS)
                nc.vector.tensor_tensor(out=q_grp[:, cols, :], in0=bank[:], in1=m_rep[:, cols, :], op=ADD)

        def add_plain(c, half):
            family = c // PASSES_PER_FAMILY
            m_half = m_banks[family] if c < STAGED_PASSES else m_rows[(family, half)]
            q_sum = halves.tile([P, PACK, D_TILE], BF16)
            nc.vector.tensor_tensor(
                out=q_sum[:],
                in0=q_cols(c, half * D_TILE, D_TILE),
                in1=m_half[:].unsqueeze(1).to_broadcast([P, PACK, D_TILE]),
                op=ADD,
            )
            return half, q_sum

        def regroup_g(c, gpsimd_cols):
            g_raw = g_tiles[c]
            g_grp = grouped_pool.tile([P, E, PACK], BF16, align_bytes=64)
            rest = E - gpsimd_cols
            regroup(nc.scalar.copy, g_grp[:, :rest, :], g_raw[:, :, :rest], SCALAR_RUN)
            if gpsimd_cols > 0:
                nc.gpsimd.tensor_scalar(
                    out=g_grp[:, rest:, :],
                    in0=g_raw[:, :, rest:].rearrange("p j c -> p c j"),
                    scalar1=1.0,
                    scalar2=0.0,
                    op0=MULT,
                    op1=ADD,
                )
            return g_grp

        def regroup_ahead(step):
            c, first = divmod(step * AHEAD_COLS, E)
            c += STAGED_PASSES
            if first == 0:
                g_late[c] = consts.tile([P, E, PACK], BF16, align_bytes=64, name="spare_%d" % (c - STAGED_PASSES))
            cols = slice(first, first + AHEAD_COLS)
            regroup(nc.scalar.copy, g_late[c][:, cols, :], g_tiles[c][:, :, cols], SCALAR_RUN)

        def regroup_q(q_grp, q_sums, vector_cols):
            for half, q_sum in q_sums:
                share = max(0, min(D_TILE, vector_cols - half * D_TILE))
                first = half * D_TILE
                if share < D_TILE:
                    regroup(nc.scalar.copy, q_grp[:, first + share : first + D_TILE, :], q_sum[:, :, share:], SCALAR_RUN)
                if share > 0:
                    regroup(nc.vector.tensor_copy, q_grp[:, first : first + share, :], q_sum[:, :, :share], RUN)

        def quantise(c, label, grouped, width, fp8_x4, first):
            if (label, c) not in codes:
                slot = c % STAGED_PASSES
                code = keep.tile([P, width], U32, align_bytes=64, name="%s_codes_%d" % (label, slot))
                scale = keep.tile([P, width], U8, align_bytes=64, name="%s_scales_%d" % (label, slot))
                codes[(label, c)] = (code, scale)
            code, scale = codes[(label, c)]
            cols = slice(first, first + D_TILE)
            nc.vector.quantize_mx(
                out=code[:, cols].bitcast(fp8_x4),
                scales=scale[:, cols],
                in_=grouped[:, cols, :].rearrange("p c j -> p (c j)"),
            )

        def quantise_g(c, g_grp):
            quantise(c, "g", g_grp, E, E5M2_X4, 0)

        def quantise_q(c, q_grp, half):
            quantise(c, "q", q_grp, D, E4M3_X4, half * D_TILE)

        def multiply(c, tiles):
            g_codes, g_scales = codes[("g", c)]
            q_codes, q_scales = codes[("q", c)]
            for ei, di in tiles:
                d_cols = slice(di * D_TILE, (di + 1) * D_TILE)
                e_cols = slice(ei * E_TILE, (ei + 1) * E_TILE)
                nc.tensor.matmul_mx(
                    out=acc[(ei, di)][:],
                    lhsT=g_codes[:, e_cols].bitcast(E5M2_X4),
                    lhsT_scale=g_scales[:, e_cols],
                    rhs=q_codes[:, d_cols].bitcast(E4M3_X4),
                    rhs_scale=q_scales[:, d_cols],
                    start=(c == 0),
                    stop=(c == PASSES - 1),
                )

        def sums_of(c, banks):
            q_grp = grouped_pool.tile([P, D, PACK], BF16, align_bytes=64)
            if c < STAGED_PASSES:
                add_staged(c, banks, q_grp)
                if c + 1 < STAGED_PASSES:
                    banks = stage(c + 1)
                q_sums = [add_plain(c, 1)]
                if c + 1 < STAGED_PASSES and (c + 1) % PASSES_PER_FAMILY == 0:
                    stage_motion((c + 1) // PASSES_PER_FAMILY)
                if c + 1 == STAGED_PASSES:
                    for bank, tile in enumerate(DEFERRED):
                        acc[tile] = sums.tile([E_TILE, D_TILE], F32, name="late_%d" % bank)
                quantise_q(c, q_grp, 0)
            else:
                q_sums = [add_plain(c, half) for half in range(D_TILES)]
            return q_grp, q_sums, banks

        with tc.manual_schedule():
            for family in range(STAGED_FAMILIES):
                load_motion(family, 0)
            load_query(0, consts, [(0, BANK_COLS), (BANK_COLS, BANK_COLS)])
            load_motion(0, 1)
            load_query(0, consts, [(D_TILE, D_TILE)])
            load_query(1, consts, [(0, D_TILE)])
            load_grad(0)
            load_query(1, consts, [(D_TILE, D_TILE)])
            for c in range(2, LOAD_AHEAD):
                load(c)
            repeat_motion(0, [("vector", D_TILE)])
            repeat_motion(2, [("scalar", D_TILE)])
            repeat_motion(1, [("gpsimd", D_TILE // 2), ("scalar", D_TILE // 2)])
            banks = stage(0)
            stage_motion(0)
            q_grp, q_sums, banks = sums_of(0, banks)
            g_grp = regroup_g(0, 0)
            late_done = 0
            for c in range(PASSES):
                if c + LOAD_AHEAD <= PASSES:
                    load(c + LOAD_AHEAD)
                steps_a_pass = E // AHEAD_COLS
                ahead_step = c - AHEAD_FIRST
                if 0 <= ahead_step + 2 < (PASSES - STAGED_PASSES) * steps_a_pass and (ahead_step + 2) % steps_a_pass == 0:
                    load_grad(STAGED_PASSES + (ahead_step + 2) // steps_a_pass)
                staged = c < STAGED_PASSES
                if staged:
                    vector_cols = 0
                elif c + 1 < PASSES:
                    vector_cols = VECTOR_COLS_PLAIN
                else:
                    vector_cols = D_TILE
                regroup_q(q_grp, q_sums, vector_cols)
                q_grp_now, g_grp_now = q_grp, g_grp
                if c + 1 < PASSES:
                    if c + 1 < STAGED_PASSES:
                        g_grp = regroup_g(c + 1, GPSIMD_COLS)
                    else:
                        g_grp = g_late[c + 1]
                    if 0 <= ahead_step < (PASSES - STAGED_PASSES) * steps_a_pass:
                        regroup_ahead(ahead_step)
                    q_grp, q_sums, banks = sums_of(c + 1, banks)
                tiles = early_tiles
                if c + 2 >= STAGED_PASSES:
                    behind = range(late_done, min(late_done + CATCH_UP, c))
                    for past in behind:
                        multiply(past, DEFERRED)
                    late_done = max(late_done, behind.stop)
                    if late_done == c:
                        tiles = out_tiles
                        late_done = c + 1
                if c + 2 < STAGED_PASSES:
                    quantise_q(c, q_grp_now, 1)
                    quantise_g(c, g_grp_now)
                else:
                    quantise_g(c, g_grp_now)
                    if not staged:
                        quantise_q(c, q_grp_now, 0)
                    quantise_q(c, q_grp_now, 1)
                multiply(c, tiles)

            for di in range(D_TILES):
                res = loads.tile([E_TILE, E_TILES, D_TILE], F32, align_bytes=64, name="q_raw")
                for ei in range(E_TILES):
                    if ei % 2 == 0:
                        nc.vector.tensor_copy(out=res[:, ei, :], in_=acc[(ei, di)][:])
                    else:
                        nc.scalar.copy(out=res[:, ei, :], in_=acc[(ei, di)][:])
                    nc.sync.dma_start(
                        out=out[ei * E_TILE : (ei + 1) * E_TILE, di * D_TILE : (di + 1) * D_TILE],
                        in_=res[:, ei, :],
                    )
